import numpy as np
import ml_dtypes


def mxq(x, axis, fmt="e4m3"):
    dtype, down = {"e4m3": (ml_dtypes.float8_e4m3fn, 7), "e5m2": (ml_dtypes.float8_e5m2, 14)}[fmt]
    v = np.moveaxis(np.asarray(x, np.float32).astype(ml_dtypes.bfloat16).astype(np.float64), axis, -1)
    blocks = v.reshape(v.shape[:-1] + (-1, 32))
    amax = np.abs(blocks).max(-1, keepdims=True)
    byte = np.maximum(np.where(amax > 0, np.frexp(amax)[1] - 1 + 127, 0) - down, 1)
    scale = np.exp2(byte - 127.0)
    codes = (blocks / scale).astype(np.float32).astype(dtype).astype(np.float64)
    return np.moveaxis((codes * scale).reshape(v.shape), -1, axis)


WIDE = False


def mx_kscale(k):
    if not WIDE:
        return np.ones(k)
    levels = np.array([20, -20, 10, -10, 0])
    a = np.random.permutation(np.resize(levels, k // 512 * 4)).reshape(k // 512, 4)
    idx = np.arange(k)
    return np.exp2(a[idx // 512, idx % 128 // 32])


BF16 = ml_dtypes.bfloat16


def bf(x):
    return np.asarray(x, np.float32).astype(BF16)


def f64(x):
    return np.asarray(x).astype(np.float64)


B, N, F, O, E, K = 4, 128, 256, 32, 16, 3


def setup_inputs():
    se = np.asarray(mx_kscale(E * O)).reshape(E, O)[:, 0]
    x_g = np.random.standard_normal((B, K, N, F))
    emb = np.random.standard_normal((B, N, E)) * se
    weights_pool = np.random.standard_normal((E, K, F, O)) * 0.5 / np.sqrt(K * F) / se[:, None, None, None]
    bias_pool = np.random.standard_normal((E, O)) * 0.3 / se[:, None]
    g = np.random.standard_normal((B, N, O)) * np.exp2(np.random.randint(-12, 1, (B, N, 1))) * 64.0
    return {"x_g": bf(x_g), "emb": bf(emb), "weights_pool": bf(weights_pool), "bias_pool": bf(bias_pool),
            "grad_out": bf(g)}


def reference(x_g, emb, weights_pool, bias_pool, grad_out):
    e, w, g = f64(emb), f64(weights_pool), f64(grad_out)
    gz = (e[:, :, :, None] * g[:, :, None, :]).reshape(B * N, E * O)
    wt = w.transpose(1, 2, 0, 3).reshape(K * F, E * O)
    gx = mxq(gz, 1, "e5m2") @ mxq(wt, 1, "e4m3").T
    return gx.reshape(B, N, K, F).transpose(0, 2, 1, 3)

@@ -1,0 +1,142 @@
+from contextlib import ExitStack
+
+import concourse.mybir as mybir
+from concourse.masks import make_identity
+
+F32 = mybir.dt.float32
+BF16 = mybir.dt.bfloat16
+U32 = mybir.dt.uint32
+U8 = mybir.dt.uint8
+E4M3_X4 = mybir.dt.float8_e4m3fn_x4
+E5M2_X4 = mybir.dt.float8_e5m2_x4
+
+B, N, F, O, E, K = 4, 128, 256, 32, 16, 3
+P = 128
+PACK = 4
+R = O // PACK
+HALVES = 2
+KF = K * F
+LO = KF // P
+PASS_COLS = 512
+LO_PER_BANK = PASS_COLS // (HALVES * P)
+E_PER_LOAD = 4
+
+FLOPS = 2 * B * N * E * O * KF
+BYTES = 2 * (B * N * E + B * N * O + E * KF * O) + 4 * B * N * KF
+
+
+def tile_dygcn_pb_s_kernel(tc, x_g, emb, weights_pool, bias_pool, grad_out, out):
+    nc = tc.nc
+    with ExitStack() as ctx:
+        keep = ctx.enter_context(tc.tile_pool(name="keep", bufs=1))
+        psum = ctx.enter_context(tc.psum_pool(name="psum", bufs=8))
+
+        identity = keep.tile([P, P], F32)
+        make_identity(nc, identity[:])
+
+        emb_sb = keep.tile([P, B, E], BF16)
+        nc.sync.dma_start(out=emb_sb[:], in_=emb.rearrange("b n e -> n b e"))
+        grad_sb = keep.tile([P, B, O], BF16)
+        nc.sync.dma_start(out=grad_sb[:], in_=grad_out.rearrange("b n o -> n b o"))
+
+        w_dram = weights_pool.rearrange("e k f o -> e (k f) o").rearrange(
+            "e (h l) o -> h e (l o)", l=LO
+        )
+        w_raw = keep.tile([P, E * LO * O], BF16)
+        w_raw_by_e = w_raw[:].rearrange("h (e c) -> h e c", e=E)
+        for e0 in range(0, E, E_PER_LOAD):
+            e_range = slice(e0, e0 + E_PER_LOAD)
+            nc.sync.dma_start(out=w_raw_by_e[:, e_range, :], in_=w_dram[:, e_range, :])
+
+        gz_grouped = keep.tile([P, B, N, PACK], BF16, align_bytes=64)
+        for b in range(B):
+            gz_tokens = keep.tile([P, PACK, E, R], F32, name="gz_tokens%d" % b)
+            nc.vector.tensor_tensor(
+                out=gz_tokens[:],
+                in0=emb_sb[:, b, :].unsqueeze(1).unsqueeze(3).to_broadcast([P, PACK, E, R]),
+                in1=grad_sb[:, b, :]
+                .rearrange("n (r t) -> n t r", t=PACK)
+                .unsqueeze(2)
+                .to_broadcast([P, PACK, E, R]),
+                op=mybir.AluOpType.mult,
+            )
+            gz_bank = psum.tile([P, PACK, N], F32, tag="bank")
+            for t in range(PACK):
+                nc.tensor.transpose(
+                    gz_bank[:, t, :],
+                    gz_tokens[:, t, :, :].rearrange("n e r -> n (e r)"),
+                    identity[:],
+                )
+            nc.scalar.copy(out=gz_grouped[:, b, :, :], in_=gz_bank[:].rearrange("p t n -> p n t"))
+
+        gz_codes = keep.tile([P, B * N], U32, align_bytes=64)
+        gz_scales = keep.tile([P, B * N], U8, align_bytes=64)
+        nc.vector.quantize_mx(
+            out=gz_codes[:].bitcast(E5M2_X4),
+            scales=gz_scales[:],
+            in_=gz_grouped[:].rearrange("p b n t -> p (b n t)"),
+        )
+
+        w_words = w_raw[:].bitcast(F32).rearrange(
+            "h (e l r u) -> h l u e r", e=E, l=LO, r=R, u=HALVES
+        )
+        w_sorted = keep.tile([P, LO, HALVES, E, R], F32)
+        for e0 in range(0, E, E_PER_LOAD):
+            e_range = slice(e0, e0 + E_PER_LOAD)
+            nc.vector.tensor_copy(
+                out=w_sorted[:, :, :, e_range, :], in_=w_words[:, :, :, e_range, :]
+            )
+
+        w_grouped = keep.tile([P, KF * PACK], BF16, align_bytes=64)
+        w_grouped_words = w_grouped[:].bitcast(F32).rearrange(
+            "p (h a l u) -> p a h l u", a=LO // LO_PER_BANK, l=LO_PER_BANK, u=HALVES
+        )
+        for a in range(LO // LO_PER_BANK):
+            w_bank = psum.tile([P, LO_PER_BANK, HALVES, P], F32, tag="bank")
+            for l in range(LO_PER_BANK):
+                for u in range(HALVES):
+                    nc.tensor.transpose(
+                        w_bank[:, l, u, :],
+                        w_sorted[:, a * LO_PER_BANK + l, u, :, :].rearrange("h e r -> h (e r)"),
+                        identity[:],
+                    )
+            nc.scalar.copy(
+                out=w_grouped_words[:, a, :, :, :], in_=w_bank[:].rearrange("p l u h -> p h l u")
+            )
+
+        w_codes = keep.tile([P, KF], U32, align_bytes=64)
+        w_scales = keep.tile([P, KF], U8, align_bytes=64)
+        for kf0, kf1 in ((0, PASS_COLS), (PASS_COLS, KF)):
+            nc.vector.quantize_mx(
+                out=w_codes[:, kf0:kf1].bitcast(E4M3_X4),
+                scales=w_scales[:, kf0:kf1],
+                in_=w_grouped[:, PACK * kf0 : PACK * kf1],
+            )
+
+        for b in range(B):
+            tokens = slice(b * N, (b + 1) * N)
+            result = keep.tile([P, K, F], F32, name="result%d" % b)
+            for first_k, kept_k in ((0, 0), (1, 2)):
+                kf_range = slice(first_k * F, first_k * F + PASS_COLS)
+                acc = psum.tile([P, PASS_COLS // F, F], F32, tag="bank")
+                nc.tensor.matmul_mx(
+                    out=acc[:].rearrange("n k f -> n (k f)"),
+                    lhsT=gz_codes[:, tokens].bitcast(E5M2_X4),
+                    lhsT_scale=gz_scales[:, tokens],
+                    rhs=w_codes[:, kf_range].bitcast(E4M3_X4),
+                    rhs_scale=w_scales[:, kf_range],
+                    start=True,
+                    stop=True,
+                )
+                if (b + first_k) % 2 == 0:
+                    nc.vector.tensor_copy(
+                        out=result[:, kept_k : first_k + 2, :], in_=acc[:, kept_k - first_k :, :]
+                    )
+                else:
+                    nc.scalar.copy(
+                        out=result[:, kept_k : first_k + 2, :], in_=acc[:, kept_k - first_k :, :]
+                    )
+                nc.sync.dma_start(
+                    out=out[b, kept_k : first_k + 2, :, :].rearrange("k n f -> n k f"),
+                    in_=result[:, kept_k : first_k + 2, :],
+                )

@@ -16,10 +16,9 @@ PACK = 4
 R = O // PACK
 HALVES = 2
 KF = K * F
-LO = KF // P
 PASS_COLS = 512
-LO_PER_BANK = PASS_COLS // (HALVES * P)
-E_PER_LOAD = 4
+L_PER_BANK = PASS_COLS // (HALVES * P)
+W_PARTS = ((0, PASS_COLS), (PASS_COLS, KF))
 
 FLOPS = 2 * B * N * E * O * KF
 BYTES = 2 * (B * N * E + B * N * O + E * KF * O) + 4 * B * N * KF
@@ -39,14 +38,16 @@ def tile_dygcn_pb_s_kernel(tc, x_g, emb, weights_pool, bias_pool, grad_out, out)
         grad_sb = keep.tile([P, B, O], BF16)
         nc.sync.dma_start(out=grad_sb[:], in_=grad_out.rearrange("b n o -> n b o"))
 
-        w_dram = weights_pool.rearrange("e k f o -> e (k f) o").rearrange(
-            "e (h l) o -> h e (l o)", l=LO
-        )
-        w_raw = keep.tile([P, E * LO * O], BF16)
-        w_raw_by_e = w_raw[:].rearrange("h (e c) -> h e c", e=E)
-        for e0 in range(0, E, E_PER_LOAD):
-            e_range = slice(e0, e0 + E_PER_LOAD)
-            nc.sync.dma_start(out=w_raw_by_e[:, e_range, :], in_=w_dram[:, e_range, :])
+        w_by_column = weights_pool.rearrange("e k f o -> e (k f) o")
+        w_raw = []
+        for kf0, kf1 in W_PARTS:
+            n_l = (kf1 - kf0) // P
+            raw = keep.tile([P, E * n_l * O], BF16, name="w_raw%d" % kf0)
+            nc.sync.dma_start(
+                out=raw[:].rearrange("h (e c) -> h e c", e=E),
+                in_=w_by_column[:, kf0:kf1, :].rearrange("e (h l) o -> h e (l o)", l=n_l),
+            )
+            w_raw.append(raw)
 
         gz_grouped = keep.tile([P, B, N, PACK], BF16, align_bytes=64)
         for b in range(B):
@@ -77,47 +78,47 @@ def tile_dygcn_pb_s_kernel(tc, x_g, emb, weights_pool, bias_pool, grad_out, out)
             in_=gz_grouped[:].rearrange("p b n t -> p (b n t)"),
         )
 
-        w_words = w_raw[:].bitcast(F32).rearrange(
-            "h (e l r u) -> h l u e r", e=E, l=LO, r=R, u=HALVES
-        )
-        w_sorted = keep.tile([P, LO, HALVES, E, R], F32)
-        for e0 in range(0, E, E_PER_LOAD):
-            e_range = slice(e0, e0 + E_PER_LOAD)
-            nc.vector.tensor_copy(
-                out=w_sorted[:, :, :, e_range, :], in_=w_words[:, :, :, e_range, :]
-            )
-
         w_grouped = keep.tile([P, KF * PACK], BF16, align_bytes=64)
-        w_grouped_words = w_grouped[:].bitcast(F32).rearrange(
-            "p (h a l u) -> p a h l u", a=LO // LO_PER_BANK, l=LO_PER_BANK, u=HALVES
-        )
-        for a in range(LO // LO_PER_BANK):
-            w_bank = psum.tile([P, LO_PER_BANK, HALVES, P], F32, tag="bank")
-            for l in range(LO_PER_BANK):
-                for u in range(HALVES):
-                    nc.tensor.transpose(
-                        w_bank[:, l, u, :],
-                        w_sorted[:, a * LO_PER_BANK + l, u, :, :].rearrange("h e r -> h (e r)"),
-                        identity[:],
-                    )
-            nc.scalar.copy(
-                out=w_grouped_words[:, a, :, :, :], in_=w_bank[:].rearrange("p l u h -> p h l u")
-            )
-
         w_codes = keep.tile([P, KF], U32, align_bytes=64)
         w_scales = keep.tile([P, KF], U8, align_bytes=64)
-        for kf0, kf1 in ((0, PASS_COLS), (PASS_COLS, KF)):
+        for (kf0, kf1), raw in zip(W_PARTS, w_raw):
+            n_l = (kf1 - kf0) // P
+            w_sorted = keep.tile([P, n_l, HALVES, E, R], F32, name="w_sorted%d" % kf0)
+            nc.vector.tensor_copy(
+                out=w_sorted[:],
+                in_=raw[:]
+                .bitcast(F32)
+                .rearrange("h (e l r u) -> h l u e r", e=E, l=n_l, r=R, u=HALVES),
+            )
+            grouped_words = (
+                w_grouped[:, PACK * kf0 : PACK * kf1]
+                .bitcast(F32)
+                .rearrange("p (h a l u) -> p a h l u", a=n_l // L_PER_BANK, l=L_PER_BANK, u=HALVES)
+            )
+            for a in range(n_l // L_PER_BANK):
+                w_bank = psum.tile([P, L_PER_BANK, HALVES, P], F32, tag="bank")
+                for l in range(L_PER_BANK):
+                    for u in range(HALVES):
+                        nc.tensor.transpose(
+                            w_bank[:, l, u, :],
+                            w_sorted[:, a * L_PER_BANK + l, u, :, :].rearrange("h e r -> h (e r)"),
+                            identity[:],
+                        )
+                nc.scalar.copy(
+                    out=grouped_words[:, a, :, :, :], in_=w_bank[:].rearrange("p l u h -> p h l u")
+                )
             nc.vector.quantize_mx(
                 out=w_codes[:, kf0:kf1].bitcast(E4M3_X4),
                 scales=w_scales[:, kf0:kf1],
                 in_=w_grouped[:, PACK * kf0 : PACK * kf1],
             )
 
-        for b in range(B):
-            tokens = slice(b * N, (b + 1) * N)
-            result = keep.tile([P, K, F], F32, name="result%d" % b)
-            for first_k, kept_k in ((0, 0), (1, 2)):
-                kf_range = slice(first_k * F, first_k * F + PASS_COLS)
+        result = keep.tile([P, B, K, F], F32)
+        for first_k, kept_k in ((0, 0), (1, 2)):
+            kf_range = slice(first_k * F, first_k * F + PASS_COLS)
+            k_range = slice(kept_k, first_k + PASS_COLS // F)
+            for b in range(B):
+                tokens = slice(b * N, (b + 1) * N)
                 acc = psum.tile([P, PASS_COLS // F, F], F32, tag="bank")
                 nc.tensor.matmul_mx(
                     out=acc[:].rearrange("n k f -> n (k f)"),
@@ -128,15 +129,11 @@ def tile_dygcn_pb_s_kernel(tc, x_g, emb, weights_pool, bias_pool, grad_out, out)
                     start=True,
                     stop=True,
                 )
-                if (b + first_k) % 2 == 0:
-                    nc.vector.tensor_copy(
-                        out=result[:, kept_k : first_k + 2, :], in_=acc[:, kept_k - first_k :, :]
-                    )
+                if b % 2 == 0:
+                    nc.vector.tensor_copy(out=result[:, b, k_range, :], in_=acc[:, kept_k - first_k :, :])
                 else:
-                    nc.scalar.copy(
-                        out=result[:, kept_k : first_k + 2, :], in_=acc[:, kept_k - first_k :, :]
-                    )
+                    nc.scalar.copy(out=result[:, b, k_range, :], in_=acc[:, kept_k - first_k :, :])
                 nc.sync.dma_start(
-                    out=out[b, kept_k : first_k + 2, :, :].rearrange("k n f -> n k f"),
-                    in_=result[:, kept_k : first_k + 2, :],
+                    out=out[b, k_range, :, :].rearrange("k n f -> n k f"),
+                    in_=result[:, b, k_range, :],
                 )

@@ -33,8 +33,8 @@ def tile_dygcn_pb_s_kernel(tc, x_g, emb, weights_pool, bias_pool, grad_out, out)
         identity = keep.tile([P, P], F32)
         make_identity(nc, identity[:])
 
-        emb_sb = keep.tile([P, B, E], BF16)
-        nc.sync.dma_start(out=emb_sb[:], in_=emb.rearrange("b n e -> n b e"))
+        emb_sb = keep.tile([P, B * E], BF16)
+        nc.sync.dma_start(out=emb_sb[:].rearrange("n (b e) -> n b e", b=B), in_=emb.rearrange("b n e -> n b e"))
         grad_sb = keep.tile([P, B, O], BF16)
         nc.sync.dma_start(out=grad_sb[:], in_=grad_out.rearrange("b n o -> n b o"))
 
@@ -49,90 +49,86 @@ def tile_dygcn_pb_s_kernel(tc, x_g, emb, weights_pool, bias_pool, grad_out, out)
             )
             w_raw.append(raw)
 
+        emb_pairs = keep.tile([P, B * E, 2], BF16)
+        nc.vector.tensor_copy(out=emb_pairs[:], in_=emb_sb[:].unsqueeze(2).to_broadcast([P, B * E, 2]))
         gz_grouped = keep.tile([P, B, N, PACK], BF16, align_bytes=64)
-        for b in range(B):
-            gz_tokens = keep.tile([P, PACK, E, R], F32, name="gz_tokens%d" % b)
-            nc.vector.tensor_tensor(
-                out=gz_tokens[:],
-                in0=emb_sb[:, b, :].unsqueeze(1).unsqueeze(3).to_broadcast([P, PACK, E, R]),
-                in1=grad_sb[:, b, :]
-                .rearrange("n (r t) -> n t r", t=PACK)
-                .unsqueeze(2)
-                .to_broadcast([P, PACK, E, R]),
-                op=mybir.AluOpType.mult,
-            )
-            gz_bank = psum.tile([P, PACK, N], F32, tag="bank")
-            for t in range(PACK):
-                nc.tensor.transpose(
-                    gz_bank[:, t, :],
-                    gz_tokens[:, t, :, :].rearrange("n e r -> n (e r)"),
-                    identity[:],
-                )
-            nc.scalar.copy(out=gz_grouped[:, b, :, :], in_=gz_bank[:].rearrange("p t n -> p n t"))
-
         gz_codes = keep.tile([P, B * N], U32, align_bytes=64)
         gz_scales = keep.tile([P, B * N], U8, align_bytes=64)
-        nc.vector.quantize_mx(
-            out=gz_codes[:].bitcast(E5M2_X4),
-            scales=gz_scales[:],
-            in_=gz_grouped[:].rearrange("p b n t -> p (b n t)"),
-        )
+        for b0 in range(0, B, 2):
+            gz_bank = psum.tile([P, 2, HALVES, N], F32, tag="bank")
+            for i in range(2):
+                b = b0 + i
+                gz_tokens = keep.tile([P, E, O], BF16, name="gz_tokens%d" % b)
+                nc.vector.tensor_tensor(
+                    out=gz_tokens[:].rearrange("n e (w q) -> n e w q", q=2),
+                    in0=emb_pairs[:, b * E : (b + 1) * E, :].unsqueeze(2).to_broadcast([P, E, O // 2, 2]),
+                    in1=grad_sb[:, b, :]
+                    .rearrange("n (w q) -> n w q", q=2)
+                    .unsqueeze(1)
+                    .to_broadcast([P, E, O // 2, 2]),
+                    op=mybir.AluOpType.mult,
+                )
+                gz_words = gz_tokens[:].rearrange("n e o -> n (e o)").bitcast(F32)
+                for u in range(HALVES):
+                    nc.tensor.transpose(gz_bank[:, i, u, :], gz_words[:, u : HALVES * P : HALVES], identity[:])
+            nc.scalar.copy(
+                out=gz_grouped[:, b0 : b0 + 2, :, :]
+                .rearrange("p b n t -> p (b n t)")
+                .bitcast(F32)
+                .rearrange("p (b n u) -> p b n u", b=2, u=HALVES),
+                in_=gz_bank[:].rearrange("p b u n -> p b n u"),
+            )
+            nc.vector.quantize_mx(
+                out=gz_codes[:, b0 * N : (b0 + 2) * N].bitcast(E5M2_X4),
+                scales=gz_scales[:, b0 * N : (b0 + 2) * N],
+                in_=gz_grouped[:, b0 : b0 + 2, :, :].rearrange("p b n t -> p (b n t)"),
+            )
 
         w_grouped = keep.tile([P, KF * PACK], BF16, align_bytes=64)
         w_codes = keep.tile([P, KF], U32, align_bytes=64)
         w_scales = keep.tile([P, KF], U8, align_bytes=64)
         for (kf0, kf1), raw in zip(W_PARTS, w_raw):
             n_l = (kf1 - kf0) // P
-            w_sorted = keep.tile([P, n_l, HALVES, E, R], F32, name="w_sorted%d" % kf0)
-            nc.vector.tensor_copy(
-                out=w_sorted[:],
-                in_=raw[:]
-                .bitcast(F32)
-                .rearrange("h (e l r u) -> h l u e r", e=E, l=n_l, r=R, u=HALVES),
-            )
-            grouped_words = (
-                w_grouped[:, PACK * kf0 : PACK * kf1]
-                .bitcast(F32)
-                .rearrange("p (h a l u) -> p a h l u", a=n_l // L_PER_BANK, l=L_PER_BANK, u=HALVES)
-            )
-            for a in range(n_l // L_PER_BANK):
-                w_bank = psum.tile([P, L_PER_BANK, HALVES, P], F32, tag="bank")
-                for l in range(L_PER_BANK):
-                    for u in range(HALVES):
-                        nc.tensor.transpose(
-                            w_bank[:, l, u, :],
-                            w_sorted[:, a * L_PER_BANK + l, u, :, :].rearrange("h e r -> h (e r)"),
-                            identity[:],
-                        )
+            raw_words = raw[:].bitcast(F32).rearrange("h (e l r u) -> h l u e r", e=E, l=n_l, r=R, u=HALVES)
+            for l in range(n_l):
+                x0 = kf0 + l * P
+                w_sorted = keep.tile([P, HALVES, E, R], F32, name="w_sorted%d" % x0)
+                nc.vector.tensor_copy(out=w_sorted[:], in_=raw_words[:, l, :, :, :])
+                w_bank = psum.tile([P, HALVES, P], F32, tag="bank")
+                for u in range(HALVES):
+                    nc.tensor.transpose(
+                        w_bank[:, u, :], w_sorted[:, u, :, :].rearrange("h e r -> h (e r)"), identity[:]
+                    )
                 nc.scalar.copy(
-                    out=grouped_words[:, a, :, :, :], in_=w_bank[:].rearrange("p l u h -> p h l u")
+                    out=w_grouped[:, PACK * x0 : PACK * (x0 + P)].bitcast(F32).rearrange("p (h u) -> p h u", u=HALVES),
+                    in_=w_bank[:].rearrange("p u h -> p h u"),
                 )
-            nc.vector.quantize_mx(
-                out=w_codes[:, kf0:kf1].bitcast(E4M3_X4),
-                scales=w_scales[:, kf0:kf1],
-                in_=w_grouped[:, PACK * kf0 : PACK * kf1],
-            )
+                nc.vector.quantize_mx(
+                    out=w_codes[:, x0 : x0 + P].bitcast(E4M3_X4),
+                    scales=w_scales[:, x0 : x0 + P],
+                    in_=w_grouped[:, PACK * x0 : PACK * (x0 + P)],
+                )
 
         result = keep.tile([P, B, K, F], F32)
-        for first_k, kept_k in ((0, 0), (1, 2)):
-            kf_range = slice(first_k * F, first_k * F + PASS_COLS)
-            k_range = slice(kept_k, first_k + PASS_COLS // F)
+        for x_first, kept, n_l, k_range in ((0, 0, 4, slice(0, 2)), (F, F, 2, slice(2, 3))):
             for b in range(B):
                 tokens = slice(b * N, (b + 1) * N)
-                acc = psum.tile([P, PASS_COLS // F, F], F32, tag="bank")
+                acc = psum.tile([P, PASS_COLS], F32, tag="bank")
                 nc.tensor.matmul_mx(
-                    out=acc[:].rearrange("n k f -> n (k f)"),
+                    out=acc[:],
                     lhsT=gz_codes[:, tokens].bitcast(E5M2_X4),
                     lhsT_scale=gz_scales[:, tokens],
-                    rhs=w_codes[:, kf_range].bitcast(E4M3_X4),
-                    rhs_scale=w_scales[:, kf_range],
+                    rhs=w_codes[:, x_first : x_first + PASS_COLS].bitcast(E4M3_X4),
+                    rhs_scale=w_scales[:, x_first : x_first + PASS_COLS],
                     start=True,
                     stop=True,
                 )
+                res = result[:, b, k_range, :].rearrange("n k f -> n (k f)").rearrange("n (h l) -> n h l", l=n_l)
+                src_cols = acc[:, kept:].rearrange("n (l h) -> n h l", l=n_l)
                 if b % 2 == 0:
-                    nc.vector.tensor_copy(out=result[:, b, k_range, :], in_=acc[:, kept_k - first_k :, :])
+                    nc.vector.tensor_copy(out=res, in_=src_cols)
                 else:
-                    nc.scalar.copy(out=result[:, b, k_range, :], in_=acc[:, kept_k - first_k :, :])
+                    nc.scalar.copy(out=res, in_=src_cols)
                 nc.sync.dma_start(
                     out=out[b, k_range, :, :].rearrange("k n f -> n k f"),
                     in_=result[:, b, k_range, :],

@@ -12,6 +12,7 @@ E5M2_X4 = mybir.dt.float8_e5m2_x4
 
 B, N, F, O, E, K = 4, 128, 256, 32, 16, 3
 P = 128
+J = 4
 PACK = 4
 R = O // PACK
 HALVES = 2
@@ -33,10 +34,12 @@ def tile_dygcn_pb_s_kernel(tc, x_g, emb, weights_pool, bias_pool, grad_out, out)
         identity = keep.tile([P, P], F32)
         make_identity(nc, identity[:])
 
-        emb_sb = keep.tile([P, B * E], BF16)
-        nc.sync.dma_start(out=emb_sb[:].rearrange("n (b e) -> n b e", b=B), in_=emb.rearrange("b n e -> n b e"))
-        grad_sb = keep.tile([P, B, O], BF16)
-        nc.sync.dma_start(out=grad_sb[:], in_=grad_out.rearrange("b n o -> n b o"))
+        emb_sb = keep.tile([P, J * E], BF16)
+        nc.sync.dma_start(out=emb_sb[:], in_=emb.rearrange("b (m j) e -> (b m) (j e)", j=J))
+        grad_sb = keep.tile([P, J, O], BF16)
+        nc.sync.dma_start(
+            out=grad_sb[:].rearrange("m j o -> m (j o)"), in_=grad_out.rearrange("b (m j) o -> (b m) (j o)", j=J)
+        )
 
         w_by_column = weights_pool.rearrange("e k f o -> e (k f) o")
         w_raw = []
@@ -49,20 +52,21 @@ def tile_dygcn_pb_s_kernel(tc, x_g, emb, weights_pool, bias_pool, grad_out, out)
             )
             w_raw.append(raw)
 
-        emb_pairs = keep.tile([P, B * E, 2], BF16)
-        nc.vector.tensor_copy(out=emb_pairs[:], in_=emb_sb[:].unsqueeze(2).to_broadcast([P, B * E, 2]))
-        gz_grouped = keep.tile([P, B, N, PACK], BF16, align_bytes=64)
+        emb_pairs = keep.tile([P, J * E, 2], BF16)
+        nc.vector.tensor_copy(out=emb_pairs[:], in_=emb_sb[:].unsqueeze(2).to_broadcast([P, J * E, 2]))
+        gz_grouped = keep.tile([P, B * N * PACK], BF16, align_bytes=64)
+        gz_grouped_words = gz_grouped[:].bitcast(F32).rearrange("p (m j u) -> p m j u", j=J, u=HALVES)
         gz_codes = keep.tile([P, B * N], U32, align_bytes=64)
         gz_scales = keep.tile([P, B * N], U8, align_bytes=64)
-        for b0 in range(0, B, 2):
-            gz_bank = psum.tile([P, 2, HALVES, N], F32, tag="bank")
+        for j0 in range(0, J, 2):
+            gz_bank = psum.tile([P, 2, HALVES, P], F32, tag="bank")
             for i in range(2):
-                b = b0 + i
-                gz_tokens = keep.tile([P, E, O], BF16, name="gz_tokens%d" % b)
+                j = j0 + i
+                gz_tokens = keep.tile([P, E, O], BF16, name="gz_tokens%d" % j)
                 nc.vector.tensor_tensor(
                     out=gz_tokens[:].rearrange("n e (w q) -> n e w q", q=2),
-                    in0=emb_pairs[:, b * E : (b + 1) * E, :].unsqueeze(2).to_broadcast([P, E, O // 2, 2]),
-                    in1=grad_sb[:, b, :]
+                    in0=emb_pairs[:, j * E : (j + 1) * E, :].unsqueeze(2).to_broadcast([P, E, O // 2, 2]),
+                    in1=grad_sb[:, j, :]
                     .rearrange("n (w q) -> n w q", q=2)
                     .unsqueeze(1)
                     .to_broadcast([P, E, O // 2, 2]),
@@ -72,64 +76,78 @@ def tile_dygcn_pb_s_kernel(tc, x_g, emb, weights_pool, bias_pool, grad_out, out)
                 for u in range(HALVES):
                     nc.tensor.transpose(gz_bank[:, i, u, :], gz_words[:, u : HALVES * P : HALVES], identity[:])
             nc.scalar.copy(
-                out=gz_grouped[:, b0 : b0 + 2, :, :]
-                .rearrange("p b n t -> p (b n t)")
-                .bitcast(F32)
-                .rearrange("p (b n u) -> p b n u", b=2, u=HALVES),
-                in_=gz_bank[:].rearrange("p b u n -> p b n u"),
+                out=gz_grouped_words[:, :, j0 : j0 + 2, :], in_=gz_bank[:].rearrange("p j u m -> p m j u")
             )
+
+        def quantise_gz(b0):
             nc.vector.quantize_mx(
                 out=gz_codes[:, b0 * N : (b0 + 2) * N].bitcast(E5M2_X4),
                 scales=gz_scales[:, b0 * N : (b0 + 2) * N],
-                in_=gz_grouped[:, b0 : b0 + 2, :, :].rearrange("p b n t -> p (b n t)"),
+                in_=gz_grouped[:, b0 * N * PACK : (b0 + 2) * N * PACK],
             )
 
         w_grouped = keep.tile([P, KF * PACK], BF16, align_bytes=64)
         w_codes = keep.tile([P, KF], U32, align_bytes=64)
         w_scales = keep.tile([P, KF], U8, align_bytes=64)
-        for (kf0, kf1), raw in zip(W_PARTS, w_raw):
+
+        def turn_weights(part, l, sort_engine):
+            kf0, kf1 = W_PARTS[part]
             n_l = (kf1 - kf0) // P
-            raw_words = raw[:].bitcast(F32).rearrange("h (e l r u) -> h l u e r", e=E, l=n_l, r=R, u=HALVES)
-            for l in range(n_l):
-                x0 = kf0 + l * P
-                w_sorted = keep.tile([P, HALVES, E, R], F32, name="w_sorted%d" % x0)
+            raw_words = (
+                w_raw[part][:].bitcast(F32).rearrange("h (e l r u) -> h l u e r", e=E, l=n_l, r=R, u=HALVES)
+            )
+            x0 = kf0 + l * P
+            w_sorted = keep.tile([P, HALVES, E, R], F32, name="w_sorted%d" % x0)
+            if sort_engine == "vector":
                 nc.vector.tensor_copy(out=w_sorted[:], in_=raw_words[:, l, :, :, :])
-                w_bank = psum.tile([P, HALVES, P], F32, tag="bank")
-                for u in range(HALVES):
-                    nc.tensor.transpose(
-                        w_bank[:, u, :], w_sorted[:, u, :, :].rearrange("h e r -> h (e r)"), identity[:]
-                    )
-                nc.scalar.copy(
-                    out=w_grouped[:, PACK * x0 : PACK * (x0 + P)].bitcast(F32).rearrange("p (h u) -> p h u", u=HALVES),
-                    in_=w_bank[:].rearrange("p u h -> p h u"),
-                )
-                nc.vector.quantize_mx(
-                    out=w_codes[:, x0 : x0 + P].bitcast(E4M3_X4),
-                    scales=w_scales[:, x0 : x0 + P],
-                    in_=w_grouped[:, PACK * x0 : PACK * (x0 + P)],
-                )
+            else:
+                nc.scalar.copy(out=w_sorted[:], in_=raw_words[:, l, :, :, :])
+            w_bank = psum.tile([P, HALVES, P], F32, tag="bank")
+            for u in range(HALVES):
+                nc.tensor.transpose(w_bank[:, u, :], w_sorted[:, u, :, :].rearrange("h e r -> h (e r)"), identity[:])
+            nc.scalar.copy(
+                out=w_grouped[:, PACK * x0 : PACK * (x0 + P)].bitcast(F32).rearrange("p (h u) -> p h u", u=HALVES),
+                in_=w_bank[:].rearrange("p u h -> p h u"),
+            )
+
+        def quantise_weights(x0):
+            nc.vector.quantize_mx(
+                out=w_codes[:, x0 : x0 + P].bitcast(E4M3_X4),
+                scales=w_scales[:, x0 : x0 + P],
+                in_=w_grouped[:, PACK * x0 : PACK * (x0 + P)],
+            )
 
         result = keep.tile([P, B, K, F], F32)
-        for x_first, kept, n_l, k_range in ((0, 0, 4, slice(0, 2)), (F, F, 2, slice(2, 3))):
-            for b in range(B):
-                tokens = slice(b * N, (b + 1) * N)
-                acc = psum.tile([P, PASS_COLS], F32, tag="bank")
-                nc.tensor.matmul_mx(
-                    out=acc[:],
-                    lhsT=gz_codes[:, tokens].bitcast(E5M2_X4),
-                    lhsT_scale=gz_scales[:, tokens],
-                    rhs=w_codes[:, x_first : x_first + PASS_COLS].bitcast(E4M3_X4),
-                    rhs_scale=w_scales[:, x_first : x_first + PASS_COLS],
-                    start=True,
-                    stop=True,
-                )
-                res = result[:, b, k_range, :].rearrange("n k f -> n (k f)").rearrange("n (h l) -> n h l", l=n_l)
-                src_cols = acc[:, kept:].rearrange("n (l h) -> n h l", l=n_l)
+
+        def product(which, b):
+            x_first, kept, n_l, k_range = ((0, 0, 4, slice(0, 2)), (F, F, 2, slice(2, 3)))[which]
+            tokens = slice(b * N, (b + 1) * N)
+            acc = psum.tile([P, PASS_COLS], F32, tag="bank")
+            nc.tensor.matmul_mx(
+                out=acc[:],
+                lhsT=gz_codes[:, tokens].bitcast(E5M2_X4),
+                lhsT_scale=gz_scales[:, tokens],
+                rhs=w_codes[:, x_first : x_first + PASS_COLS].bitcast(E4M3_X4),
+                rhs_scale=w_scales[:, x_first : x_first + PASS_COLS],
+                start=True,
+                stop=True,
+            )
+            src_cols = acc[:, kept:].rearrange("n (l h) -> n h l", l=n_l)
+            h_per_k = F // n_l
+            for i, k in enumerate(range(k_range.start, k_range.stop)):
+                res = result[:, b, k, :].rearrange("n (h l) -> n h l", l=n_l)
                 if b % 2 == 0:
-                    nc.vector.tensor_copy(out=res, in_=src_cols)
+                    nc.vector.tensor_copy(out=res, in_=src_cols[:, i * h_per_k : (i + 1) * h_per_k, :])
                 else:
-                    nc.scalar.copy(out=res, in_=src_cols)
-                nc.sync.dma_start(
-                    out=out[b, k_range, :, :].rearrange("k n f -> n k f"),
-                    in_=result[:, b, k_range, :],
-                )
+                    nc.scalar.copy(out=res, in_=src_cols[:, i * h_per_k : (i + 1) * h_per_k, :])
+                nc.sync.dma_start(out=out[b, k, :, :], in_=result[:, b, k, :])
+
+        quantise_gz(0)
+        quantise_gz(2)
+        for part, n_l in ((0, 4), (1, 2)):
+            for l in range(n_l):
+                turn_weights(part, l, "vector")
+                quantise_weights(W_PARTS[part][0] + l * P)
+        for which in range(2):
+            for b in range(B):
+                product(which, b)

@@ -12,6 +12,7 @@ E5M2_X4 = mybir.dt.float8_e5m2_x4
 
 B, N, F, O, E, K = 4, 128, 256, 32, 16, 3
 P = 128
+WARM_UPS = 4
 J = 4
 PACK = 4
 R = O // PACK
@@ -33,6 +34,10 @@ def tile_dygcn_pb_s_kernel(tc, x_g, emb, weights_pool, bias_pool, grad_out, out)
 
         identity = keep.tile([P, P], F32)
         make_identity(nc, identity[:])
+
+        warm = psum.tile([P, P], F32, tag="bank")
+        for i in range(WARM_UPS):
+            nc.tensor.matmul(out=warm[:], lhsT=identity[:], rhs=identity[:], start=True, stop=True)
 
         emb_sb = keep.tile([P, J * E], BF16)
         nc.sync.dma_start(out=emb_sb[:], in_=emb.rearrange("b (m j) e -> (b m) (j e)", j=J))

@@ -36,8 +36,12 @@ def tile_dygcn_pb_s_kernel(tc, x_g, emb, weights_pool, bias_pool, grad_out, out)
         make_identity(nc, identity[:])
 
         warm = psum.tile([P, P], F32, tag="bank")
-        for i in range(WARM_UPS):
-            nc.tensor.matmul(out=warm[:], lhsT=identity[:], rhs=identity[:], start=True, stop=True)
+
+        def keep_warm(words, times):
+            for i in range(times):
+                nc.tensor.matmul(out=warm[:], lhsT=words, rhs=identity[:], start=True, stop=True)
+
+        keep_warm(identity[:], WARM_UPS)
 
         emb_sb = keep.tile([P, J * E], BF16)
         nc.sync.dma_start(out=emb_sb[:], in_=emb.rearrange("b (m j) e -> (b m) (j e)", j=J))
@@ -80,6 +84,7 @@ def tile_dygcn_pb_s_kernel(tc, x_g, emb, weights_pool, bias_pool, grad_out, out)
                 gz_words = gz_tokens[:].rearrange("n e o -> n (e o)").bitcast(F32)
                 for u in range(HALVES):
                     nc.tensor.transpose(gz_bank[:, i, u, :], gz_words[:, u : HALVES * P : HALVES], identity[:])
+            keep_warm(gz_words[:, :P], 1)
             nc.scalar.copy(
                 out=gz_grouped_words[:, :, j0 : j0 + 2, :], in_=gz_bank[:].rearrange("p j u m -> p m j u")
             )
@@ -110,6 +115,8 @@ def tile_dygcn_pb_s_kernel(tc, x_g, emb, weights_pool, bias_pool, grad_out, out)
             w_bank = psum.tile([P, HALVES, P], F32, tag="bank")
             for u in range(HALVES):
                 nc.tensor.transpose(w_bank[:, u, :], w_sorted[:, u, :, :].rearrange("h e r -> h (e r)"), identity[:])
+            if x0 == PASS_COLS - P:
+                keep_warm(w_sorted[:, 0, :, :].rearrange("h e r -> h (e r)"), 2)
             nc.scalar.copy(
                 out=w_grouped[:, PACK * x0 : PACK * (x0 + P)].bitcast(F32).rearrange("p (h u) -> p h u", u=HALVES),
                 in_=w_bank[:].rearrange("p u h -> p h u"),

@@ -31,6 +31,7 @@ def tile_dygcn_pb_s_kernel(tc, x_g, emb, weights_pool, bias_pool, grad_out, out)
     with ExitStack() as ctx:
         keep = ctx.enter_context(tc.tile_pool(name="keep", bufs=1))
         psum = ctx.enter_context(tc.psum_pool(name="psum", bufs=8))
+        ctx.enter_context(tc.manual_schedule())
 
         identity = keep.tile([P, P], F32)
         make_identity(nc, identity[:])
@@ -100,7 +101,9 @@ def tile_dygcn_pb_s_kernel(tc, x_g, emb, weights_pool, bias_pool, grad_out, out)
         w_codes = keep.tile([P, KF], U32, align_bytes=64)
         w_scales = keep.tile([P, KF], U8, align_bytes=64)
 
-        def turn_weights(part, l, sort_engine):
+        w_sorted_tiles = {}
+
+        def sort_weights(part, l, sort_engine):
             kf0, kf1 = W_PARTS[part]
             n_l = (kf1 - kf0) // P
             raw_words = (
@@ -112,6 +115,10 @@ def tile_dygcn_pb_s_kernel(tc, x_g, emb, weights_pool, bias_pool, grad_out, out)
                 nc.vector.tensor_copy(out=w_sorted[:], in_=raw_words[:, l, :, :, :])
             else:
                 nc.scalar.copy(out=w_sorted[:], in_=raw_words[:, l, :, :, :])
+            w_sorted_tiles[x0] = w_sorted
+
+        def turn_weights(x0):
+            w_sorted = w_sorted_tiles[x0]
             w_bank = psum.tile([P, HALVES, P], F32, tag="bank")
             for u in range(HALVES):
                 nc.tensor.transpose(w_bank[:, u, :], w_sorted[:, u, :, :].rearrange("h e r -> h (e r)"), identity[:])
@@ -148,18 +155,28 @@ def tile_dygcn_pb_s_kernel(tc, x_g, emb, weights_pool, bias_pool, grad_out, out)
             h_per_k = F // n_l
             for i, k in enumerate(range(k_range.start, k_range.stop)):
                 res = result[:, b, k, :].rearrange("n (h l) -> n h l", l=n_l)
-                if b % 2 == 0:
+                if b % 2 == 1:
                     nc.vector.tensor_copy(out=res, in_=src_cols[:, i * h_per_k : (i + 1) * h_per_k, :])
                 else:
                     nc.scalar.copy(out=res, in_=src_cols[:, i * h_per_k : (i + 1) * h_per_k, :])
                 nc.sync.dma_start(out=out[b, k, :, :], in_=result[:, b, k, :])
 
+        for l in range(4):
+            sort_weights(0, l, "vector")
+            turn_weights(l * P)
         quantise_gz(0)
+        for l in range(4):
+            quantise_weights(l * P)
         quantise_gz(2)
-        for part, n_l in ((0, 4), (1, 2)):
-            for l in range(n_l):
-                turn_weights(part, l, "vector")
-                quantise_weights(W_PARTS[part][0] + l * P)
-        for which in range(2):
-            for b in range(B):
-                product(which, b)
+        for l in range(2):
+            sort_weights(1, l, "scalar")
+        product(0, 0)
+        product(0, 1)
+        for l in range(2):
+            turn_weights(PASS_COLS + l * P)
+        for l in range(2):
+            quantise_weights(PASS_COLS + l * P)
+        product(0, 2)
+        product(0, 3)
+        for b in range(B):
+            product(1, b)

@@ -85,7 +85,7 @@ def tile_dygcn_pb_s_kernel(tc, x_g, emb, weights_pool, bias_pool, grad_out, out)
                 gz_words = gz_tokens[:].rearrange("n e o -> n (e o)").bitcast(F32)
                 for u in range(HALVES):
                     nc.tensor.transpose(gz_bank[:, i, u, :], gz_words[:, u : HALVES * P : HALVES], identity[:])
-            keep_warm(gz_words[:, :P], 1)
+            keep_warm(gz_words[:, :P], 1 + j0 // 2)
             nc.scalar.copy(
                 out=gz_grouped_words[:, :, j0 : j0 + 2, :], in_=gz_bank[:].rearrange("p j u m -> p m j u")
             )

@@ -13,14 +13,16 @@ E5M2_X4 = mybir.dt.float8_e5m2_x4
 B, N, F, O, E, K = 4, 128, 256, 32, 16, 3
 P = 128
 WARM_UPS = 4
-J = 4
+PAIRS = B // 2
+J = 2
 PACK = 4
-R = O // PACK
-HALVES = 2
+U = 2
+EU = E // U
+W = O // 2
+H = P // U
 KF = K * F
 PASS_COLS = 512
-L_PER_BANK = PASS_COLS // (HALVES * P)
-W_PARTS = ((0, PASS_COLS), (PASS_COLS, KF))
+W_PARTS = ((0, 2), (2, K))
 
 FLOPS = 2 * B * N * E * O * KF
 BYTES = 2 * (B * N * E + B * N * O + E * KF * O) + 4 * B * N * KF
@@ -36,6 +38,9 @@ def tile_dygcn_pb_s_kernel(tc, x_g, emb, weights_pool, bias_pool, grad_out, out)
         identity = keep.tile([P, P], F32)
         make_identity(nc, identity[:])
 
+        table_call = keep.tile([P, 1], F32)
+        nc.scalar.copy(out=table_call[:], in_=identity[:, :1])
+
         warm = psum.tile([P, P], F32, tag="bank")
 
         def keep_warm(words, times):
@@ -44,139 +49,189 @@ def tile_dygcn_pb_s_kernel(tc, x_g, emb, weights_pool, bias_pool, grad_out, out)
 
         keep_warm(identity[:], WARM_UPS)
 
-        emb_sb = keep.tile([P, J * E], BF16)
-        nc.sync.dma_start(out=emb_sb[:], in_=emb.rearrange("b (m j) e -> (b m) (j e)", j=J))
-        grad_sb = keep.tile([P, J, O], BF16)
-        nc.sync.dma_start(
-            out=grad_sb[:].rearrange("m j o -> m (j o)"), in_=grad_out.rearrange("b (m j) o -> (b m) (j o)", j=J)
-        )
+        emb_sb = keep.tile([P, PAIRS, J * E], BF16)
+        nc.sync.dma_start(out=emb_sb[:], in_=emb.rearrange("(i b) (m j) e -> (b m) i (j e)", i=PAIRS, j=J))
+        grad_sb = keep.tile([P, PAIRS, J * O], BF16)
+        nc.sync.dma_start(out=grad_sb[:], in_=grad_out.rearrange("(i b) (m j) o -> (b m) i (j o)", i=PAIRS, j=J))
 
-        w_by_column = weights_pool.rearrange("e k f o -> e (k f) o")
         w_raw = []
-        for kf0, kf1 in W_PARTS:
-            n_l = (kf1 - kf0) // P
-            raw = keep.tile([P, E * n_l * O], BF16, name="w_raw%d" % kf0)
-            nc.sync.dma_start(
-                out=raw[:].rearrange("h (e c) -> h e c", e=E),
-                in_=w_by_column[:, kf0:kf1, :].rearrange("e (h l) o -> h e (l o)", l=n_l),
-            )
+        for k0, k1 in W_PARTS:
+            n_l = (k1 - k0) * F // H
+            raw = keep.tile([P, EU, n_l * O], BF16, name="w_raw%d" % k0)
+            by_column = weights_pool[:, k0:k1, :, :].rearrange("e k f o -> e (k f) o")
+            for u in range(U):
+                nc.sync.dma_start(
+                    out=raw[u:P:U, :, :],
+                    in_=by_column[u * EU : (u + 1) * EU, :, :].rearrange("e (h l) o -> h e (l o)", l=n_l),
+                )
             w_raw.append(raw)
 
-        emb_pairs = keep.tile([P, J * E, 2], BF16)
-        nc.vector.tensor_copy(out=emb_pairs[:], in_=emb_sb[:].unsqueeze(2).to_broadcast([P, J * E, 2]))
-        gz_grouped = keep.tile([P, B * N * PACK], BF16, align_bytes=64)
-        gz_grouped_words = gz_grouped[:].bitcast(F32).rearrange("p (m j u) -> p m j u", j=J, u=HALVES)
-        gz_codes = keep.tile([P, B * N], U32, align_bytes=64)
-        gz_scales = keep.tile([P, B * N], U8, align_bytes=64)
-        for j0 in range(0, J, 2):
-            gz_bank = psum.tile([P, 2, HALVES, P], F32, tag="bank")
-            for i in range(2):
-                j = j0 + i
-                gz_tokens = keep.tile([P, E, O], BF16, name="gz_tokens%d" % j)
-                nc.vector.tensor_tensor(
-                    out=gz_tokens[:].rearrange("n e (w q) -> n e w q", q=2),
-                    in0=emb_pairs[:, j * E : (j + 1) * E, :].unsqueeze(2).to_broadcast([P, E, O // 2, 2]),
-                    in1=grad_sb[:, j, :]
-                    .rearrange("n (w q) -> n w q", q=2)
-                    .unsqueeze(1)
-                    .to_broadcast([P, E, O // 2, 2]),
-                    op=mybir.AluOpType.mult,
-                )
-                gz_words = gz_tokens[:].rearrange("n e o -> n (e o)").bitcast(F32)
-                for u in range(HALVES):
-                    nc.tensor.transpose(gz_bank[:, i, u, :], gz_words[:, u : HALVES * P : HALVES], identity[:])
-            keep_warm(gz_words[:, :P], 1 + j0 // 2)
-            nc.scalar.copy(
-                out=gz_grouped_words[:, :, j0 : j0 + 2, :], in_=gz_bank[:].rearrange("p j u m -> p m j u")
-            )
-
-        def quantise_gz(b0):
-            nc.vector.quantize_mx(
-                out=gz_codes[:, b0 * N : (b0 + 2) * N].bitcast(E5M2_X4),
-                scales=gz_scales[:, b0 * N : (b0 + 2) * N],
-                in_=gz_grouped[:, b0 * N * PACK : (b0 + 2) * N * PACK],
-            )
-
-        w_grouped = keep.tile([P, KF * PACK], BF16, align_bytes=64)
         w_codes = keep.tile([P, KF], U32, align_bytes=64)
         w_scales = keep.tile([P, KF], U8, align_bytes=64)
 
-        w_sorted_tiles = {}
+        emb_pairs = keep.tile([P, PAIRS * J * E, 2], BF16)
+        gz_grouped = keep.tile([P, B * N * PACK], BF16, align_bytes=64)
+        gz_codes = keep.tile([P, B * N], U32, align_bytes=64)
+        gz_scales = keep.tile([P, B * N], U8, align_bytes=64)
+        gz_tokens = {}
+        gz_banks = {}
 
-        def sort_weights(part, l, sort_engine):
-            kf0, kf1 = W_PARTS[part]
-            n_l = (kf1 - kf0) // P
-            raw_words = (
-                w_raw[part][:].bitcast(F32).rearrange("h (e l r u) -> h l u e r", e=E, l=n_l, r=R, u=HALVES)
+        def double_emb():
+            nc.vector.tensor_copy(
+                out=emb_pairs[:],
+                in_=emb_sb[:].rearrange("m i c -> m (i c)").unsqueeze(2).to_broadcast([P, PAIRS * J * E, 2]),
             )
-            x0 = kf0 + l * P
-            w_sorted = keep.tile([P, HALVES, E, R], F32, name="w_sorted%d" % x0)
-            if sort_engine == "vector":
-                nc.vector.tensor_copy(out=w_sorted[:], in_=raw_words[:, l, :, :, :])
+
+        def multiply_gz(i, j):
+            tokens = keep.tile([P, E, O], BF16, name="gz_tokens%d%d" % (i, j))
+            first = (i * J + j) * E
+            nc.vector.tensor_tensor(
+                out=tokens[:].rearrange("n e (w q) -> n e w q", q=2),
+                in0=emb_pairs[:, first : first + E, :].unsqueeze(2).to_broadcast([P, E, W, 2]),
+                in1=grad_sb[:, i, j * O : (j + 1) * O]
+                .rearrange("n (w q) -> n w q", q=2)
+                .unsqueeze(1)
+                .to_broadcast([P, E, W, 2]),
+                op=mybir.AluOpType.mult,
+            )
+            gz_tokens[i, j] = tokens
+
+        def turn_gz(i, j):
+            if j == 0:
+                gz_banks[i] = psum.tile([P, J, U, P], F32, tag="bank", name="gz_bank%d" % i)
+            words = gz_tokens[i, j][:].rearrange("n e o -> n (e o)").bitcast(F32)
+            for u in range(U):
+                nc.tensor.transpose(gz_banks[i][:, j, u, :], words[:, u * P : (u + 1) * P], identity[:])
+
+        def copy_gz(i, engine):
+            half = slice(i * 2 * N * PACK, (i + 1) * 2 * N * PACK)
+            words = gz_grouped[:, half].bitcast(F32).rearrange("p (m j u) -> p m j u", j=J, u=U)
+            turned = gz_banks[i][:].rearrange("p j u m -> p m j u")
+            if engine == "vector":
+                nc.vector.tensor_copy(out=words, in_=turned)
             else:
-                nc.scalar.copy(out=w_sorted[:], in_=raw_words[:, l, :, :, :])
-            w_sorted_tiles[x0] = w_sorted
+                nc.scalar.copy(out=words, in_=turned)
 
-        def turn_weights(x0):
-            w_sorted = w_sorted_tiles[x0]
-            w_bank = psum.tile([P, HALVES, P], F32, tag="bank")
-            for u in range(HALVES):
-                nc.tensor.transpose(w_bank[:, u, :], w_sorted[:, u, :, :].rearrange("h e r -> h (e r)"), identity[:])
-            if x0 == PASS_COLS - P:
-                keep_warm(w_sorted[:, 0, :, :].rearrange("h e r -> h (e r)"), 2)
-            nc.scalar.copy(
-                out=w_grouped[:, PACK * x0 : PACK * (x0 + P)].bitcast(F32).rearrange("p (h u) -> p h u", u=HALVES),
-                in_=w_bank[:].rearrange("p u h -> p h u"),
+        def quantise_gz(i):
+            cols = slice(i * 2 * N, (i + 1) * 2 * N)
+            nc.vector.quantize_mx(
+                out=gz_codes[:, cols].bitcast(E5M2_X4),
+                scales=gz_scales[:, cols],
+                in_=gz_grouped[:, i * 2 * N * PACK : (i + 1) * 2 * N * PACK],
             )
 
-        def quantise_weights(x0):
+        w_sorted = {}
+        w_banks = {}
+        w_grouped = {}
+
+        def sort_weights(part, l0, l1, engine):
+            k0, k1 = W_PARTS[part]
+            n_l = (k1 - k0) * F // H
+            words = w_raw[part][:].bitcast(F32).rearrange("p e (l w) -> p l e w", l=n_l)
+            w_sorted[part, l0] = keep.tile([P, l1 - l0, EU, W], F32, name="w_sorted%d%d" % (part, l0))
+            if engine == "vector":
+                nc.vector.tensor_copy(out=w_sorted[part, l0][:], in_=words[:, l0:l1, :, :])
+            else:
+                nc.scalar.copy(out=w_sorted[part, l0][:], in_=words[:, l0:l1, :, :])
+
+        def turn_weights(part, l0, l1, s0):
+            bank = psum.tile([P, l1 - l0, P], F32, tag="bank", name="w_bank%d%d" % (part, l0))
+            for l in range(l0, l1):
+                nc.tensor.transpose(
+                    bank[:, l - l0, :], w_sorted[part, s0][:, l - s0, :, :].rearrange("h e w -> h (e w)"), identity[:]
+                )
+            w_banks[part, l0] = bank
+
+        def copy_weights(part, l0, l1, engine):
+            grouped = keep.tile([P, (l1 - l0) * P * 2], BF16, align_bytes=64, name="w_grouped%d%d" % (part, l0))
+            w_grouped[part, l0] = grouped
+            words = w_banks[part, l0][:].rearrange("p l h -> p (l h)")
+            if engine == "vector":
+                nc.vector.tensor_copy(out=grouped[:].bitcast(F32), in_=words)
+            else:
+                nc.scalar.copy(out=grouped[:].bitcast(F32), in_=words)
+
+        def quantise_weights(part, l0, l1):
+            x0 = W_PARTS[part][0] * F
+            cols = slice(x0 + l0 * H, x0 + l1 * H)
             nc.vector.quantize_mx(
-                out=w_codes[:, x0 : x0 + P].bitcast(E4M3_X4),
-                scales=w_scales[:, x0 : x0 + P],
-                in_=w_grouped[:, PACK * x0 : PACK * (x0 + P)],
+                out=w_codes[:, cols].bitcast(E4M3_X4),
+                scales=w_scales[:, cols],
+                in_=w_grouped[part, l0][:],
             )
 
         result = keep.tile([P, B, K, F], F32)
+        accs = {}
 
-        def product(which, b):
-            x_first, kept, n_l, k_range = ((0, 0, 4, slice(0, 2)), (F, F, 2, slice(2, 3)))[which]
+        def product(part, b):
             tokens = slice(b * N, (b + 1) * N)
-            acc = psum.tile([P, PASS_COLS], F32, tag="bank")
+            window = slice(W_PARTS[part][1] * F - PASS_COLS, W_PARTS[part][1] * F)
+            acc = psum.tile([P, PASS_COLS], F32, tag="bank", name="acc%d%d" % (part, b))
             nc.tensor.matmul_mx(
                 out=acc[:],
                 lhsT=gz_codes[:, tokens].bitcast(E5M2_X4),
                 lhsT_scale=gz_scales[:, tokens],
-                rhs=w_codes[:, x_first : x_first + PASS_COLS].bitcast(E4M3_X4),
-                rhs_scale=w_scales[:, x_first : x_first + PASS_COLS],
+                rhs=w_codes[:, window].bitcast(E4M3_X4),
+                rhs_scale=w_scales[:, window],
                 start=True,
                 stop=True,
             )
-            src_cols = acc[:, kept:].rearrange("n (l h) -> n h l", l=n_l)
-            h_per_k = F // n_l
-            for i, k in enumerate(range(k_range.start, k_range.stop)):
-                res = result[:, b, k, :].rearrange("n (h l) -> n h l", l=n_l)
-                if b % 2 == 1:
-                    nc.vector.tensor_copy(out=res, in_=src_cols[:, i * h_per_k : (i + 1) * h_per_k, :])
-                else:
-                    nc.scalar.copy(out=res, in_=src_cols[:, i * h_per_k : (i + 1) * h_per_k, :])
-                nc.sync.dma_start(out=out[b, k, :, :], in_=result[:, b, k, :])
+            accs[part, b] = acc
 
-        for l in range(4):
-            sort_weights(0, l, "vector")
-            turn_weights(l * P)
+        def leave(part, b, engine):
+            k0, k1 = W_PARTS[part]
+            n_l = (k1 - k0) * F // H
+            n_h = F // n_l
+            used = accs[part, b][:, PASS_COLS - (k1 - k0) * F :].rearrange("n (l h) -> n h l", l=n_l)
+            for k in range(k0, k1):
+                cols = used[:, (k - k0) * n_h : (k - k0 + 1) * n_h, :]
+                res = result[:, b, k, :].rearrange("n (h l) -> n h l", l=n_l)
+                if engine == "vector":
+                    nc.vector.tensor_copy(out=res, in_=cols)
+                else:
+                    nc.scalar.copy(out=res, in_=cols)
+                if part == 0:
+                    nc.sync.dma_start(out=out[b, k, :, :], in_=result[:, b, k, :])
+                elif b % 2 == 1:
+                    nc.sync.dma_start(
+                        out=out[b - 1 : b + 1, k, :, :].rearrange("b n f -> n b f"), in_=result[:, b - 1 : b + 1, k, :]
+                    )
+
+        double_emb()
+        multiply_gz(0, 0)
+        multiply_gz(0, 1)
+        multiply_gz(1, 0)
+        for j in range(J):
+            turn_gz(0, j)
+        copy_gz(0, "scalar")
+        for l in range(0, 8, 2):
+            sort_weights(0, l, l + 2, "vector")
+            turn_weights(0, l, l + 2, l)
+        multiply_gz(1, 1)
+        for l in range(0, 8, 2):
+            copy_weights(0, l, l + 2, "vector" if l == 0 else "scalar")
         quantise_gz(0)
-        for l in range(4):
-            quantise_weights(l * P)
-        quantise_gz(2)
-        for l in range(2):
-            sort_weights(1, l, "scalar")
+        for l in range(0, 8, 2):
+            quantise_weights(0, l, l + 2)
+        for j in range(J):
+            turn_gz(1, j)
+        keep_warm(identity[:], 2)
+        copy_gz(1, "scalar")
+        for l in (0, 2):
+            sort_weights(1, l, l + 2, "vector")
+        quantise_gz(1)
         product(0, 0)
+        for l in (0, 2):
+            turn_weights(1, l, l + 2, l)
+            copy_weights(1, l, l + 2, "vector")
+            quantise_weights(1, l, l + 2)
         product(0, 1)
-        for l in range(2):
-            turn_weights(PASS_COLS + l * P)
-        for l in range(2):
-            quantise_weights(PASS_COLS + l * P)
+        leave(0, 0, "scalar")
+        leave(0, 1, "scalar")
         product(0, 2)
         product(0, 3)
+        leave(0, 2, "scalar")
+        leave(0, 3, "scalar")
         for b in range(B):
             product(1, b)
+            leave(1, b, ("vector", "scalar")[b % 2])

@@ -145,11 +145,12 @@ def tile_dygcn_pb_s_kernel(tc, x_g, emb, weights_pool, bias_pool, grad_out, out)
         def copy_weights(part, l0, l1, engine):
             grouped = keep.tile([P, (l1 - l0) * P * 2], BF16, align_bytes=64, name="w_grouped%d%d" % (part, l0))
             w_grouped[part, l0] = grouped
-            words = w_banks[part, l0][:].rearrange("p l h -> p (l h)")
+            words = grouped[:].bitcast(F32).rearrange("p (h l u) -> p h l u", l=l1 - l0, u=U)
+            turned = w_banks[part, l0][:].rearrange("p l (h u) -> p h l u", u=U)
             if engine == "vector":
-                nc.vector.tensor_copy(out=grouped[:].bitcast(F32), in_=words)
+                nc.vector.tensor_copy(out=words, in_=turned)
             else:
-                nc.scalar.copy(out=grouped[:].bitcast(F32), in_=words)
+                nc.scalar.copy(out=words, in_=turned)
 
         def quantise_weights(part, l0, l1):
             x0 = W_PARTS[part][0] * F
@@ -182,10 +183,10 @@ def tile_dygcn_pb_s_kernel(tc, x_g, emb, weights_pool, bias_pool, grad_out, out)
             k0, k1 = W_PARTS[part]
             n_l = (k1 - k0) * F // H
             n_h = F // n_l
-            used = accs[part, b][:, PASS_COLS - (k1 - k0) * F :].rearrange("n (l h) -> n h l", l=n_l)
+            used = accs[part, b][:, PASS_COLS - (k1 - k0) * F :].rearrange("n (g h l) -> n h g l", h=H, l=2)
             for k in range(k0, k1):
-                cols = used[:, (k - k0) * n_h : (k - k0 + 1) * n_h, :]
-                res = result[:, b, k, :].rearrange("n (h l) -> n h l", l=n_l)
+                cols = used[:, (k - k0) * n_h : (k - k0 + 1) * n_h, :, :]
+                res = result[:, b, k, :].rearrange("n (h g l) -> n h g l", g=n_l // 2, l=2)
                 if engine == "vector":
                     nc.vector.tensor_copy(out=res, in_=cols)
                 else:
@@ -203,6 +204,7 @@ def tile_dygcn_pb_s_kernel(tc, x_g, emb, weights_pool, bias_pool, grad_out, out)
         multiply_gz(1, 0)
         for j in range(J):
             turn_gz(0, j)
+        keep_warm(identity[:], 1)
         copy_gz(0, "scalar")
         for l in range(0, 8, 2):
             sort_weights(0, l, l + 2, "vector")
@@ -221,11 +223,12 @@ def tile_dygcn_pb_s_kernel(tc, x_g, emb, weights_pool, bias_pool, grad_out, out)
             sort_weights(1, l, l + 2, "vector")
         quantise_gz(1)
         product(0, 0)
+        product(0, 1)
         for l in (0, 2):
             turn_weights(1, l, l + 2, l)
             copy_weights(1, l, l + 2, "vector")
+        for l in (0, 2):
             quantise_weights(1, l, l + 2)
-        product(0, 1)
         leave(0, 0, "scalar")
         leave(0, 1, "scalar")
         product(0, 2)

@@ -22,7 +22,8 @@ W = O // 2
 H = P // U
 KF = K * F
 PASS_COLS = 512
-W_PARTS = ((0, 2), (2, K))
+PAD = PASS_COLS - F
+L = F // H
 
 FLOPS = 2 * B * N * E * O * KF
 BYTES = 2 * (B * N * E + B * N * O + E * KF * O) + 4 * B * N * KF
@@ -55,19 +56,19 @@ def tile_dygcn_pb_s_kernel(tc, x_g, emb, weights_pool, bias_pool, grad_out, out)
         nc.sync.dma_start(out=grad_sb[:], in_=grad_out.rearrange("(i b) (m j) o -> (b m) i (j o)", i=PAIRS, j=J))
 
         w_raw = []
-        for k0, k1 in W_PARTS:
-            n_l = (k1 - k0) * F // H
-            raw = keep.tile([P, EU, n_l * O], BF16, name="w_raw%d" % k0)
-            by_column = weights_pool[:, k0:k1, :, :].rearrange("e k f o -> e (k f) o")
+        for k in range(K):
+            raw = keep.tile([P, EU, L * O], BF16, name="w_raw%d" % k)
             for u in range(U):
                 nc.sync.dma_start(
                     out=raw[u:P:U, :, :],
-                    in_=by_column[u * EU : (u + 1) * EU, :, :].rearrange("e (h l) o -> h e (l o)", l=n_l),
+                    in_=weights_pool[u * EU : (u + 1) * EU, k, :, :].rearrange("e (h l) o -> h e (l o)", l=L),
                 )
             w_raw.append(raw)
 
-        w_codes = keep.tile([P, KF], U32, align_bytes=64)
-        w_scales = keep.tile([P, KF], U8, align_bytes=64)
+        w_codes = keep.tile([P, PAD + KF], U32, align_bytes=64)
+        w_scales = keep.tile([P, PAD + KF], U8, align_bytes=64)
+        nc.gpsimd.memset(w_codes[:, :PAD], 0)
+        nc.gpsimd.memset(w_scales[:, :PAD].bitcast(U32), 0)
 
         emb_pairs = keep.tile([P, PAIRS * J * E, 2], BF16)
         gz_grouped = keep.tile([P, B * N * PACK], BF16, align_bytes=64)
@@ -103,71 +104,66 @@ def tile_dygcn_pb_s_kernel(tc, x_g, emb, weights_pool, bias_pool, grad_out, out)
             for u in range(U):
                 nc.tensor.transpose(gz_banks[i][:, j, u, :], words[:, u * P : (u + 1) * P], identity[:])
 
-        def copy_gz(i, engine):
-            half = slice(i * 2 * N * PACK, (i + 1) * 2 * N * PACK)
-            words = gz_grouped[:, half].bitcast(F32).rearrange("p (m j u) -> p m j u", j=J, u=U)
-            turned = gz_banks[i][:].rearrange("p j u m -> p m j u")
+        def copy_gz(b, engine):
+            i, half = divmod(b, 2)
+            words = gz_grouped[:, b * N * PACK : (b + 1) * N * PACK].bitcast(F32)
+            words = words.rearrange("p (m j u) -> p m j u", j=J, u=U)
+            turned = gz_banks[i][:, :, :, half * (P // 2) : (half + 1) * (P // 2)].rearrange("p j u m -> p m j u")
             if engine == "vector":
                 nc.vector.tensor_copy(out=words, in_=turned)
             else:
                 nc.scalar.copy(out=words, in_=turned)
 
-        def quantise_gz(i):
-            cols = slice(i * 2 * N, (i + 1) * 2 * N)
+        def quantise_gz(b):
+            cols = slice(b * N, (b + 1) * N)
             nc.vector.quantize_mx(
                 out=gz_codes[:, cols].bitcast(E5M2_X4),
                 scales=gz_scales[:, cols],
-                in_=gz_grouped[:, i * 2 * N * PACK : (i + 1) * 2 * N * PACK],
+                in_=gz_grouped[:, b * N * PACK : (b + 1) * N * PACK],
             )
 
         w_sorted = {}
         w_banks = {}
         w_grouped = {}
 
-        def sort_weights(part, l0, l1, engine):
-            k0, k1 = W_PARTS[part]
-            n_l = (k1 - k0) * F // H
-            words = w_raw[part][:].bitcast(F32).rearrange("p e (l w) -> p l e w", l=n_l)
-            w_sorted[part, l0] = keep.tile([P, l1 - l0, EU, W], F32, name="w_sorted%d%d" % (part, l0))
-            if engine == "vector":
-                nc.vector.tensor_copy(out=w_sorted[part, l0][:], in_=words[:, l0:l1, :, :])
-            else:
-                nc.scalar.copy(out=w_sorted[part, l0][:], in_=words[:, l0:l1, :, :])
+        def sort_weights(k, g):
+            words = w_raw[k][:].bitcast(F32).rearrange("p e (l w) -> p l e w", l=L)
+            w_sorted[k, g] = keep.tile([P, 2, EU, W], F32, name="w_sorted%d%d" % (k, g))
+            nc.vector.tensor_copy(out=w_sorted[k, g][:], in_=words[:, 2 * g : 2 * g + 2, :, :])
 
-        def turn_weights(part, l0, l1, s0):
-            bank = psum.tile([P, l1 - l0, P], F32, tag="bank", name="w_bank%d%d" % (part, l0))
-            for l in range(l0, l1):
+        def turn_weights(k, g):
+            bank = psum.tile([P, 2, P], F32, tag="bank", name="w_bank%d%d" % (k, g))
+            for l in range(2):
                 nc.tensor.transpose(
-                    bank[:, l - l0, :], w_sorted[part, s0][:, l - s0, :, :].rearrange("h e w -> h (e w)"), identity[:]
+                    bank[:, l, :], w_sorted[k, g][:, l, :, :].rearrange("h e w -> h (e w)"), identity[:]
                 )
-            w_banks[part, l0] = bank
+            w_banks[k, g] = bank
 
-        def copy_weights(part, l0, l1, engine):
-            grouped = keep.tile([P, (l1 - l0) * P * 2], BF16, align_bytes=64, name="w_grouped%d%d" % (part, l0))
-            w_grouped[part, l0] = grouped
-            words = grouped[:].bitcast(F32).rearrange("p (h l u) -> p h l u", l=l1 - l0, u=U)
-            turned = w_banks[part, l0][:].rearrange("p l (h u) -> p h l u", u=U)
+        def copy_weights(k, g, engine):
+            grouped = keep.tile([P, 2 * P * 2], BF16, align_bytes=64, name="w_grouped%d%d" % (k, g))
+            w_grouped[k, g] = grouped
+            words = grouped[:].bitcast(F32).rearrange("p (h l u) -> p h l u", l=2, u=U)
+            turned = w_banks[k, g][:].rearrange("p l (h u) -> p h l u", u=U)
             if engine == "vector":
                 nc.vector.tensor_copy(out=words, in_=turned)
             else:
                 nc.scalar.copy(out=words, in_=turned)
 
-        def quantise_weights(part, l0, l1):
-            x0 = W_PARTS[part][0] * F
-            cols = slice(x0 + l0 * H, x0 + l1 * H)
+        def quantise_weights(k, g):
+            x0 = PAD + k * F + g * 2 * H
             nc.vector.quantize_mx(
-                out=w_codes[:, cols].bitcast(E4M3_X4),
-                scales=w_scales[:, cols],
-                in_=w_grouped[part, l0][:],
+                out=w_codes[:, x0 : x0 + 2 * H].bitcast(E4M3_X4),
+                scales=w_scales[:, x0 : x0 + 2 * H],
+                in_=w_grouped[k, g][:],
             )
 
         result = keep.tile([P, B, K, F], F32)
         accs = {}
 
-        def product(part, b):
+        def product(k, b):
             tokens = slice(b * N, (b + 1) * N)
-            window = slice(W_PARTS[part][1] * F - PASS_COLS, W_PARTS[part][1] * F)
-            acc = psum.tile([P, PASS_COLS], F32, tag="bank", name="acc%d%d" % (part, b))
+            window = slice(k * F, k * F + PASS_COLS)
+            acc = psum.tile([P, PASS_COLS], F32, tag="bank", name="acc%d%d" % (k, b))
             nc.tensor.matmul_mx(
                 out=acc[:],
                 lhsT=gz_codes[:, tokens].bitcast(E5M2_X4),
@@ -177,64 +173,65 @@ def tile_dygcn_pb_s_kernel(tc, x_g, emb, weights_pool, bias_pool, grad_out, out)
                 start=True,
                 stop=True,
             )
-            accs[part, b] = acc
+            accs[k, b] = acc
 
-        def leave(part, b, engine):
-            k0, k1 = W_PARTS[part]
-            n_l = (k1 - k0) * F // H
-            n_h = F // n_l
-            used = accs[part, b][:, PASS_COLS - (k1 - k0) * F :].rearrange("n (g h l) -> n h g l", h=H, l=2)
-            for k in range(k0, k1):
-                cols = used[:, (k - k0) * n_h : (k - k0 + 1) * n_h, :, :]
-                res = result[:, b, k, :].rearrange("n (h g l) -> n h g l", g=n_l // 2, l=2)
-                if engine == "vector":
-                    nc.vector.tensor_copy(out=res, in_=cols)
-                else:
-                    nc.scalar.copy(out=res, in_=cols)
-                if part == 0:
-                    nc.sync.dma_start(out=out[b, k, :, :], in_=result[:, b, k, :])
-                elif b % 2 == 1:
-                    nc.sync.dma_start(
-                        out=out[b - 1 : b + 1, k, :, :].rearrange("b n f -> n b f"), in_=result[:, b - 1 : b + 1, k, :]
-                    )
+        def leave(k, b):
+            nc.scalar.copy(
+                out=result[:, b, k, :].rearrange("n (h g l) -> n h g l", g=L // 2, l=2),
+                in_=accs[k, b][:, PAD:].rearrange("n (g h l) -> n h g l", h=H, l=2),
+            )
+            if k < K - 1:
+                nc.sync.dma_start(out=out[b, k, :, :], in_=result[:, b, k, :])
+            elif b % 2 == 1:
+                nc.sync.dma_start(
+                    out=out[b - 1 : b + 1, k, :, :].rearrange("b n f -> n b f"), in_=result[:, b - 1 : b + 1, k, :]
+                )
 
         double_emb()
-        multiply_gz(0, 0)
-        multiply_gz(0, 1)
-        multiply_gz(1, 0)
         for j in range(J):
+            multiply_gz(0, j)
             turn_gz(0, j)
         keep_warm(identity[:], 1)
         copy_gz(0, "scalar")
-        for l in range(0, 8, 2):
-            sort_weights(0, l, l + 2, "vector")
-            turn_weights(0, l, l + 2, l)
-        multiply_gz(1, 1)
-        for l in range(0, 8, 2):
-            copy_weights(0, l, l + 2, "vector" if l == 0 else "scalar")
-        quantise_gz(0)
-        for l in range(0, 8, 2):
-            quantise_weights(0, l, l + 2)
+        for g in range(2):
+            sort_weights(0, g)
+            turn_weights(0, g)
         for j in range(J):
+            multiply_gz(1, j)
             turn_gz(1, j)
+        for g in range(2):
+            sort_weights(1, g)
+            turn_weights(1, g)
         keep_warm(identity[:], 2)
-        copy_gz(1, "scalar")
-        for l in (0, 2):
-            sort_weights(1, l, l + 2, "vector")
+        copy_weights(0, 0, "vector")
+        copy_weights(0, 1, "scalar")
+        quantise_gz(0)
+        for g in range(2):
+            quantise_weights(0, g)
+        for b in range(1, B):
+            copy_gz(b, "scalar")
         quantise_gz(1)
-        product(0, 0)
-        product(0, 1)
-        for l in (0, 2):
-            turn_weights(1, l, l + 2, l)
-            copy_weights(1, l, l + 2, "vector")
-        for l in (0, 2):
-            quantise_weights(1, l, l + 2)
-        leave(0, 0, "scalar")
-        leave(0, 1, "scalar")
-        product(0, 2)
-        product(0, 3)
-        leave(0, 2, "scalar")
-        leave(0, 3, "scalar")
+        for g in range(2):
+            sort_weights(2, g)
+        copy_weights(1, 0, "vector")
+        copy_weights(1, 1, "scalar")
+        for b in range(2, B):
+            quantise_gz(b)
+        for b in range(B):
+            if b == 2:
+                for g in range(2):
+                    turn_weights(2, g)
+            product(0, b)
+            leave(0, b)
+        for g in range(2):
+            quantise_weights(1, g)
         for b in range(B):
             product(1, b)
-            leave(1, b, ("vector", "scalar")[b % 2])
+            leave(1, b)
+        for g in range(2):
+            copy_weights(2, g, "vector")
+        for g in range(2):
+            quantise_weights(2, g)
+        for b in range(B):
+            product(2, b)
+            leave(2, b)

@@ -126,10 +126,12 @@ def tile_dygcn_pb_s_kernel(tc, x_g, emb, weights_pool, bias_pool, grad_out, out)
         w_banks = {}
         w_grouped = {}
 
-        def sort_weights(k, g):
+        def sort_weights(k, g0, times):
             words = w_raw[k][:].bitcast(F32).rearrange("p e (l w) -> p l e w", l=L)
-            w_sorted[k, g] = keep.tile([P, 2, EU, W], F32, name="w_sorted%d%d" % (k, g))
-            nc.vector.tensor_copy(out=w_sorted[k, g][:], in_=words[:, 2 * g : 2 * g + 2, :, :])
+            by_l = keep.tile([P, 2 * times, EU, W], F32, name="w_sorted%d%d" % (k, g0))
+            nc.vector.tensor_copy(out=by_l[:], in_=words[:, 2 * g0 : 2 * (g0 + times), :, :])
+            for i in range(times):
+                w_sorted[k, g0 + i] = by_l[:, 2 * i : 2 * i + 2, :, :]
 
         def turn_weights(k, g):
             bank = psum.tile([P, 2, P], F32, tag="bank", name="w_bank%d%d" % (k, g))
@@ -160,10 +162,10 @@ def tile_dygcn_pb_s_kernel(tc, x_g, emb, weights_pool, bias_pool, grad_out, out)
         result = keep.tile([P, B, K, F], F32)
         accs = {}
 
-        def product(k, b):
+        def product(k1, b):
             tokens = slice(b * N, (b + 1) * N)
-            window = slice(k * F, k * F + PASS_COLS)
-            acc = psum.tile([P, PASS_COLS], F32, tag="bank", name="acc%d%d" % (k, b))
+            window = slice(k1 * F, k1 * F + PASS_COLS)
+            acc = psum.tile([P, PASS_COLS], F32, tag="bank", name="acc%d%d" % (k1, b))
             nc.tensor.matmul_mx(
                 out=acc[:],
                 lhsT=gz_codes[:, tokens].bitcast(E5M2_X4),
@@ -173,65 +175,82 @@ def tile_dygcn_pb_s_kernel(tc, x_g, emb, weights_pool, bias_pool, grad_out, out)
                 start=True,
                 stop=True,
             )
-            accs[k, b] = acc
+            accs[k1, b] = acc
 
-        def leave(k, b):
-            nc.scalar.copy(
-                out=result[:, b, k, :].rearrange("n (h g l) -> n h g l", g=L // 2, l=2),
-                in_=accs[k, b][:, PAD:].rearrange("n (g h l) -> n h g l", h=H, l=2),
-            )
-            if k < K - 1:
-                nc.sync.dma_start(out=out[b, k, :, :], in_=result[:, b, k, :])
-            elif b % 2 == 1:
-                nc.sync.dma_start(
-                    out=out[b - 1 : b + 1, k, :, :].rearrange("b n f -> n b f"), in_=result[:, b - 1 : b + 1, k, :]
-                )
+        def leave(k1, b, ks, engine):
+            for k in ks:
+                half = slice((k - k1 + 1) * F, (k - k1 + 2) * F)
+                res = result[:, b, k, :].rearrange("n (h g l) -> n h g l", g=L // 2, l=2)
+                used = accs[k1, b][:, half].rearrange("n (g h l) -> n h g l", h=H, l=2)
+                if engine == "vector":
+                    nc.vector.tensor_copy(out=res, in_=used)
+                else:
+                    nc.scalar.copy(out=res, in_=used)
+
+        def store(b, k0, k1):
+            if k1 == k0 + 1:
+                nc.sync.dma_start(out=out[b, k0, :, :], in_=result[:, b, k0, :])
+            else:
+                nc.sync.dma_start(out=out[b, k0:k1, :, :].rearrange("k n f -> n k f"), in_=result[:, b, k0:k1, :])
 
         double_emb()
         for j in range(J):
             multiply_gz(0, j)
             turn_gz(0, j)
-        keep_warm(identity[:], 1)
         copy_gz(0, "scalar")
+        multiply_gz(1, 0)
         for g in range(2):
-            sort_weights(0, g)
+            sort_weights(0, g, 1)
             turn_weights(0, g)
+        keep_warm(identity[:], 1)
+        multiply_gz(1, 1)
         for j in range(J):
-            multiply_gz(1, j)
             turn_gz(1, j)
+        keep_warm(identity[:], 1)
         for g in range(2):
-            sort_weights(1, g)
+            sort_weights(1, g, 1)
             turn_weights(1, g)
-        keep_warm(identity[:], 2)
-        copy_weights(0, 0, "vector")
+        copy_weights(0, 0, "scalar")
         copy_weights(0, 1, "scalar")
         quantise_gz(0)
         for g in range(2):
             quantise_weights(0, g)
-        for b in range(1, B):
+        for b in range(1, 3):
             copy_gz(b, "scalar")
+        copy_weights(1, 0, "scalar")
+        copy_gz(3, "scalar")
         quantise_gz(1)
-        for g in range(2):
-            sort_weights(2, g)
-        copy_weights(1, 0, "vector")
-        copy_weights(1, 1, "scalar")
-        for b in range(2, B):
-            quantise_gz(b)
-        for b in range(B):
-            if b == 2:
-                for g in range(2):
-                    turn_weights(2, g)
+        sort_weights(2, 0, 2)
+        copy_weights(1, 1, "vector")
+        quantise_gz(2)
+        for b in range(2):
             product(0, b)
-            leave(0, b)
+            leave(0, b, (0,), "scalar")
+            store(b, 0, 1)
+        for g in range(2):
+            turn_weights(2, g)
         for g in range(2):
             quantise_weights(1, g)
-        for b in range(B):
-            product(1, b)
-            leave(1, b)
+        quantise_gz(3)
         for g in range(2):
             copy_weights(2, g, "vector")
         for g in range(2):
             quantise_weights(2, g)
-        for b in range(B):
-            product(2, b)
-            leave(2, b)
+        product(1, 2)
+        for k in range(2):
+            leave(1, 2, (k,), "scalar")
+            store(2, k, k + 1)
+        product(1, 3)
+        leave(1, 3, (0, 1), "scalar")
+        store(3, 0, 2)
+        product(2, 0)
+        leave(2, 0, (1, 2), "vector")
+        store(0, 1, 3)
+        product(2, 1)
+        leave(2, 1, (1, 2), "scalar")
+        store(1, 1, 3)
+        product(2, 2)
+        leave(2, 2, (2,), "vector")
+        product(2, 3)
+        leave(2, 3, (2,), "vector")
+        nc.sync.dma_start(out=out[2:4, 2, :, :].rearrange("b n f -> n b f"), in_=result[:, 2:4, 2, :])

from contextlib import ExitStack

import concourse.mybir as mybir
from concourse.masks import make_identity

F32 = mybir.dt.float32
BF16 = mybir.dt.bfloat16
U32 = mybir.dt.uint32
U8 = mybir.dt.uint8
E4M3_X4 = mybir.dt.float8_e4m3fn_x4
E5M2_X4 = mybir.dt.float8_e5m2_x4

B, N, F, O, E, K = 4, 128, 256, 32, 16, 3
P = 128
WARM_UPS = 4
PAIRS = B // 2
J = 2
PACK = 4
U = 2
EU = E // U
W = O // 2
H = P // U
KF = K * F
PASS_COLS = 512
PAD = PASS_COLS - F
L = F // H

FLOPS = 2 * B * N * E * O * KF
BYTES = 2 * (B * N * E + B * N * O + E * KF * O) + 4 * B * N * KF


def tile_dygcn_pb_s_kernel(tc, x_g, emb, weights_pool, bias_pool, grad_out, out):
    nc = tc.nc
    with ExitStack() as ctx:
        keep = ctx.enter_context(tc.tile_pool(name="keep", bufs=1))
        psum = ctx.enter_context(tc.psum_pool(name="psum", bufs=8))
        ctx.enter_context(tc.manual_schedule())

        identity = keep.tile([P, P], F32)
        make_identity(nc, identity[:])

        table_call = keep.tile([P, 1], F32)
        nc.scalar.copy(out=table_call[:], in_=identity[:, :1])

        warm = psum.tile([P, P], F32, tag="bank")

        def keep_warm(words, times):
            for i in range(times):
                nc.tensor.matmul(out=warm[:], lhsT=words, rhs=identity[:], start=True, stop=True)

        keep_warm(identity[:], WARM_UPS)

        emb_sb = keep.tile([P, PAIRS, J * E], BF16)
        nc.sync.dma_start(out=emb_sb[:], in_=emb.rearrange("(i b) (m j) e -> (b m) i (j e)", i=PAIRS, j=J))
        grad_sb = keep.tile([P, PAIRS, J * O], BF16)
        nc.sync.dma_start(out=grad_sb[:], in_=grad_out.rearrange("(i b) (m j) o -> (b m) i (j o)", i=PAIRS, j=J))

        w_raw = []
        for k in range(K):
            raw = keep.tile([P, EU, L * O], BF16, name="w_raw%d" % k)
            for u in range(U):
                nc.sync.dma_start(
                    out=raw[u:P:U, :, :],
                    in_=weights_pool[u * EU : (u + 1) * EU, k, :, :].rearrange("e (h l) o -> h e (l o)", l=L),
                )
            w_raw.append(raw)

        w_codes = keep.tile([P, PAD + KF], U32, align_bytes=64)
        w_scales = keep.tile([P, PAD + KF], U8, align_bytes=64)
        nc.gpsimd.memset(w_codes[:, :PAD], 0)
        nc.gpsimd.memset(w_scales[:, :PAD].bitcast(U32), 0)

        emb_pairs = keep.tile([P, PAIRS * J * E, 2], BF16)
        gz_grouped = keep.tile([P, B * N * PACK], BF16, align_bytes=64)
        gz_codes = keep.tile([P, B * N], U32, align_bytes=64)
        gz_scales = keep.tile([P, B * N], U8, align_bytes=64)
        gz_tokens = {}
        gz_banks = {}

        def double_emb():
            nc.vector.tensor_copy(
                out=emb_pairs[:],
                in_=emb_sb[:].rearrange("m i c -> m (i c)").unsqueeze(2).to_broadcast([P, PAIRS * J * E, 2]),
            )

        def multiply_gz(i, j):
            tokens = keep.tile([P, E, O], BF16, name="gz_tokens%d%d" % (i, j))
            first = (i * J + j) * E
            nc.vector.tensor_tensor(
                out=tokens[:].rearrange("n e (w q) -> n e w q", q=2),
                in0=emb_pairs[:, first : first + E, :].unsqueeze(2).to_broadcast([P, E, W, 2]),
                in1=grad_sb[:, i, j * O : (j + 1) * O]
                .rearrange("n (w q) -> n w q", q=2)
                .unsqueeze(1)
                .to_broadcast([P, E, W, 2]),
                op=mybir.AluOpType.mult,
            )
            gz_tokens[i, j] = tokens

        def turn_gz(i, j):
            if j == 0:
                gz_banks[i] = psum.tile([P, J, U, P], F32, tag="bank", name="gz_bank%d" % i)
            words = gz_tokens[i, j][:].rearrange("n e o -> n (e o)").bitcast(F32)
            for u in range(U):
                nc.tensor.transpose(gz_banks[i][:, j, u, :], words[:, u * P : (u + 1) * P], identity[:])

        def copy_gz(b, engine):
            i, half = divmod(b, 2)
            words = gz_grouped[:, b * N * PACK : (b + 1) * N * PACK].bitcast(F32)
            words = words.rearrange("p (m j u) -> p m j u", j=J, u=U)
            turned = gz_banks[i][:, :, :, half * (P // 2) : (half + 1) * (P // 2)].rearrange("p j u m -> p m j u")
            if engine == "vector":
                nc.vector.tensor_copy(out=words, in_=turned)
            else:
                nc.scalar.copy(out=words, in_=turned)

        def quantise_gz(b):
            cols = slice(b * N, (b + 1) * N)
            nc.vector.quantize_mx(
                out=gz_codes[:, cols].bitcast(E5M2_X4),
                scales=gz_scales[:, cols],
                in_=gz_grouped[:, b * N * PACK : (b + 1) * N * PACK],
            )

        w_sorted = {}
        w_banks = {}
        w_grouped = {}

        def sort_weights(k, g0, times):
            words = w_raw[k][:].bitcast(F32).rearrange("p e (l w) -> p l e w", l=L)
            by_l = keep.tile([P, 2 * times, EU, W], F32, name="w_sorted%d%d" % (k, g0))
            nc.vector.tensor_copy(out=by_l[:], in_=words[:, 2 * g0 : 2 * (g0 + times), :, :])
            for i in range(times):
                w_sorted[k, g0 + i] = by_l[:, 2 * i : 2 * i + 2, :, :]

        def turn_weights(k, g):
            bank = psum.tile([P, 2, P], F32, tag="bank", name="w_bank%d%d" % (k, g))
            for l in range(2):
                nc.tensor.transpose(
                    bank[:, l, :], w_sorted[k, g][:, l, :, :].rearrange("h e w -> h (e w)"), identity[:]
                )
            w_banks[k, g] = bank

        def copy_weights(k, g, engine):
            grouped = keep.tile([P, 2 * P * 2], BF16, align_bytes=64, name="w_grouped%d%d" % (k, g))
            w_grouped[k, g] = grouped
            words = grouped[:].bitcast(F32).rearrange("p (h l u) -> p h l u", l=2, u=U)
            turned = w_banks[k, g][:].rearrange("p l (h u) -> p h l u", u=U)
            if engine == "vector":
                nc.vector.tensor_copy(out=words, in_=turned)
            else:
                nc.scalar.copy(out=words, in_=turned)

        def quantise_weights(k, g):
            x0 = PAD + k * F + g * 2 * H
            nc.vector.quantize_mx(
                out=w_codes[:, x0 : x0 + 2 * H].bitcast(E4M3_X4),
                scales=w_scales[:, x0 : x0 + 2 * H],
                in_=w_grouped[k, g][:],
            )

        result = keep.tile([P, B, K, F], F32)
        accs = {}

        def product(k1, b):
            tokens = slice(b * N, (b + 1) * N)
            window = slice(k1 * F, k1 * F + PASS_COLS)
            acc = psum.tile([P, PASS_COLS], F32, tag="bank", name="acc%d%d" % (k1, b))
            nc.tensor.matmul_mx(
                out=acc[:],
                lhsT=gz_codes[:, tokens].bitcast(E5M2_X4),
                lhsT_scale=gz_scales[:, tokens],
                rhs=w_codes[:, window].bitcast(E4M3_X4),
                rhs_scale=w_scales[:, window],
                start=True,
                stop=True,
            )
            accs[k1, b] = acc

        def leave(k1, b, ks, engine):
            for k in ks:
                half = slice((k - k1 + 1) * F, (k - k1 + 2) * F)
                res = result[:, b, k, :].rearrange("n (h g l) -> n h g l", g=L // 2, l=2)
                used = accs[k1, b][:, half].rearrange("n (g h l) -> n h g l", h=H, l=2)
                if engine == "vector":
                    nc.vector.tensor_copy(out=res, in_=used)
                else:
                    nc.scalar.copy(out=res, in_=used)

        def store(b, k0, k1):
            if k1 == k0 + 1:
                nc.sync.dma_start(out=out[b, k0, :, :], in_=result[:, b, k0, :])
            else:
                nc.sync.dma_start(out=out[b, k0:k1, :, :].rearrange("k n f -> n k f"), in_=result[:, b, k0:k1, :])

        double_emb()
        for j in range(J):
            multiply_gz(0, j)
            turn_gz(0, j)
        copy_gz(0, "scalar")
        multiply_gz(1, 0)
        for g in range(2):
            sort_weights(0, g, 1)
            turn_weights(0, g)
        keep_warm(identity[:], 1)
        multiply_gz(1, 1)
        for j in range(J):
            turn_gz(1, j)
        keep_warm(identity[:], 1)
        for g in range(2):
            sort_weights(1, g, 1)
            turn_weights(1, g)
        copy_weights(0, 0, "scalar")
        copy_weights(0, 1, "scalar")
        quantise_gz(0)
        for g in range(2):
            quantise_weights(0, g)
        for b in range(1, 3):
            copy_gz(b, "scalar")
        copy_weights(1, 0, "scalar")
        copy_gz(3, "scalar")
        quantise_gz(1)
        sort_weights(2, 0, 2)
        copy_weights(1, 1, "vector")
        quantise_gz(2)
        for b in range(2):
            product(0, b)
            leave(0, b, (0,), "scalar")
            store(b, 0, 1)
        for g in range(2):
            turn_weights(2, g)
        for g in range(2):
            quantise_weights(1, g)
        quantise_gz(3)
        for g in range(2):
            copy_weights(2, g, "vector")
        for g in range(2):
            quantise_weights(2, g)
        product(1, 2)
        for k in range(2):
            leave(1, 2, (k,), "scalar")
            store(2, k, k + 1)
        product(1, 3)
        leave(1, 3, (0, 1), "scalar")
        store(3, 0, 2)
        product(2, 0)
        leave(2, 0, (1, 2), "vector")
        store(0, 1, 3)
        product(2, 1)
        leave(2, 1, (1, 2), "scalar")
        store(1, 1, 3)
        product(2, 2)
        leave(2, 2, (2,), "vector")
        product(2, 3)
        leave(2, 3, (2,), "vector")
        nc.sync.dma_start(out=out[2:4, 2, :, :].rearrange("b n f -> n b f"), in_=result[:, 2:4, 2, :])
